import numpy as np
import ml_dtypes


def mxq(x, axis, fmt="e4m3"):
    dtype, down = {"e4m3": (ml_dtypes.float8_e4m3fn, 7), "e5m2": (ml_dtypes.float8_e5m2, 14)}[fmt]
    v = np.moveaxis(np.asarray(x, np.float32).astype(ml_dtypes.bfloat16).astype(np.float64), axis, -1)
    blocks = v.reshape(v.shape[:-1] + (-1, 32))
    amax = np.abs(blocks).max(-1, keepdims=True)
    byte = np.maximum(np.where(amax > 0, np.frexp(amax)[1] - 1 + 127, 0) - down, 1)
    scale = np.exp2(byte - 127.0)
    codes = (blocks / scale).astype(np.float32).astype(dtype).astype(np.float64)
    return np.moveaxis((codes * scale).reshape(v.shape), -1, axis)


WIDE = False


def mx_kscale(k):
    if not WIDE:
        return np.ones(k)
    levels = np.array([10, -10, 5, -5, 0])
    a = np.random.permutation(np.resize(levels, k // 512 * 4)).reshape(k // 512, 4)
    idx = np.arange(k)
    return np.exp2(a[idx // 512, idx % 128 // 32])


BF16 = ml_dtypes.bfloat16


def bf(x):
    return np.asarray(x, np.float32).astype(BF16)


def f64(x):
    return np.asarray(x).astype(np.float64)


E2M1 = np.array([0.0, 0.5, 1.0, 1.5, 2.0, 3.0, 4.0, 6.0, -0.0, -0.5, -1.0, -1.5, -2.0, -3.0, -4.0, -6.0])


def pack_weight(w, fmt):
    k, n = w.shape
    w = f64(bf(w)).reshape(k // 32, 32, n)
    amax = np.abs(w).max(1)
    if fmt == "e4m3":
        byte = np.frexp(amax)[1] - 1 + 127 - 7
    else:
        mant, ex = np.frexp(amax / 6.0)
        byte = np.where(mant > 0.5, ex, ex - 1) + 127
    byte = np.clip(np.where(amax > 0, byte, 1), 1, 254)
    scaled = (w * np.exp2(127.0 - byte)[:, None, :]).reshape(k, n).astype(np.float32)
    by_word = np.ascontiguousarray(scaled.reshape(k // 512, 128, 4, n).transpose(0, 1, 3, 2))
    if fmt == "e4m3":
        words = by_word.astype(ml_dtypes.float8_e4m3fn).view(np.uint8)
    else:
        c = by_word.astype(ml_dtypes.float4_e2m1fn).view(np.uint8) & 0xF
        words = c[..., 0::2] | (c[..., 1::2] << 4)
    return np.ascontiguousarray(words), np.ascontiguousarray(byte.astype(np.uint8).reshape(k // 512, 16, n))


def unpack_weight(words, scales, fmt):
    g, p, n, _ = words.shape
    if fmt == "e4m3":
        vals = np.ascontiguousarray(words).view(ml_dtypes.float8_e4m3fn).astype(np.float64)
    else:
        nib = np.empty((g, p, n, 4), np.uint8)
        nib[..., 0::2] = words & 0xF
        nib[..., 1::2] = words >> 4
        vals = E2M1[nib]
    vals = vals * np.repeat(np.exp2(scales.astype(np.float64) - 127.0), 8, axis=1)[..., None]
    return vals.transpose(0, 1, 3, 2).reshape(g * 512, n)


B, S, L, C, K0, K1, K2, NC = 4, 128, 512, 8, 512, 512, 16, 10
T = S * L
R = B * S
FMT = "e4m3"


def setup_inputs():
    t = mx_kscale(K0)
    level = np.random.standard_normal((B, S, C))
    x = np.random.standard_normal((B, S, L, C)) + 0.5 * level[:, :, None, :]
    w0 = np.random.standard_normal((C, L, K0)) / np.sqrt(L) * t
    b0 = bf(np.random.standard_normal((C, K0)) * 0.3 * t)
    w1 = np.random.standard_normal((C, K0, K1)) * 1.4 / np.sqrt(K0) / t[:, None]
    b1 = bf(np.random.standard_normal((C, K1)) * 0.3)
    W0_words, W0_scales = pack_weight(w0.reshape(-1, K0), FMT)
    W1_words, W1_scales = pack_weight(w1.reshape(-1, K1), FMT)
    return {"x": bf(x.reshape(B, T, C)),
            "W0_words": W0_words,
            "W0_scales": W0_scales,
            "b0": b0,
            "W1_words": W1_words,
            "W1_scales": W1_scales,
            "b1": b1}


def reference(x, W0_words, W0_scales, b0, W1_words, W1_scales, b1):
    xc = f64(x).reshape(B, S, L, C)
    mid = (xc.min(axis=2) + xc.max(axis=2)) * 0.5
    norm = xc - mid[:, :, None, :]
    nt = norm.transpose(3, 0, 1, 2).reshape(C, R, L)
    h0 = np.maximum((mxq(nt, 2, "e4m3") @ unpack_weight(W0_words, W0_scales, FMT).reshape(C, L, K0)) + f64(b0)[:, None, :], 0.0)
    h1 = np.maximum((mxq(h0, 2, "e4m3") @ unpack_weight(W1_words, W1_scales, FMT).reshape(C, K0, K1)) + f64(b1)[:, None, :], 0.0)
    return h1.reshape(C, B, S, K1).transpose(1, 2, 0, 3)

@@ -1,0 +1,270 @@
+from contextlib import ExitStack
+
+import concourse.mybir as mybir
+from concourse.masks import make_identity
+
+BF16 = mybir.dt.bfloat16
+F32 = mybir.dt.float32
+I32 = mybir.dt.int32
+U32 = mybir.dt.uint32
+U8 = mybir.dt.uint8
+FP8X4 = mybir.dt.float8_e4m3fn_x4
+ALU = mybir.AluOpType
+ACT = mybir.ActivationFunctionType
+
+P = 128
+SERIES = 4
+CHANNELS = 8
+K = 512
+GROUP = 4
+PAIR = 2
+TREE_LEVELS = 4
+FLT_MAX = 3.4028234663852886e38
+
+FLOPS = 2 * 2 * SERIES * P * CHANNELS * K * K
+
+
+def load_weight(nc, pool, label):
+    codes = pool.tile([P, CHANNELS, K], U32, name=label + "_codes", align_bytes=64)
+    planes = pool.tile([P, CHANNELS, K], U8, name=label + "_planes", align_bytes=64)
+    nc.vector.memset(planes[:].bitcast(I32), 0)
+    return codes, planes
+
+
+def load_scale_rows(nc, planes, scales):
+    for quadrant in range(4):
+        nc.sync.dma_start(
+            out=planes[32 * quadrant : 32 * quadrant + 4, :, :].bitcast(I32),
+            in_=scales[:, 4 * quadrant : 4 * quadrant + 4, :].rearrange("g q n -> q g n").bitcast(I32),
+        )
+
+
+def load_codes(nc, codes, words, first):
+    nc.sync.dma_start(
+        out=codes[:, first : first + GROUP, :].bitcast(I32),
+        in_=words[first : first + GROUP].rearrange("g p n t -> p g (n t)").bitcast(I32),
+    )
+
+
+def load_bias(nc, pool, bias, label):
+    spread = pool.tile([P, CHANNELS, K], BF16, name=label)
+    nc.sync.dma_start(
+        out=spread[:].rearrange("p c k -> p (c k)"),
+        in_=bias.rearrange("c k -> (c k)").partition_broadcast(P),
+    )
+    return spread
+
+
+def negative_midpoints(nc, tree, small, x_tile):
+    high = x_tile
+    low = x_tile
+    width = K * CHANNELS
+    for level in range(TREE_LEVELS):
+        width //= 2
+        high_next = tree.tile([P, width], BF16, name="high%d" % level)
+        low_next = tree.tile([P, width], BF16, name="low%d" % level)
+        nc.vector.tensor_tensor(
+            out=high_next[:], in0=high[:, 0:width], in1=high[:, width : 2 * width], op=ALU.max
+        )
+        nc.vector.tensor_tensor(
+            out=low_next[:], in0=low[:, 0:width], in1=low[:, width : 2 * width], op=ALU.min
+        )
+        high = high_next
+        low = low_next
+    top = small.tile([P, CHANNELS], F32, name="top")
+    bottom = small.tile([P, CHANNELS], F32, name="bottom")
+    nc.vector.tensor_reduce(
+        out=top[:], in_=high[:].rearrange("p (l c) -> p c l", c=CHANNELS), axis=mybir.AxisListType.X, op=ALU.max
+    )
+    nc.vector.tensor_reduce(
+        out=bottom[:], in_=low[:].rearrange("p (l c) -> p c l", c=CHANNELS), axis=mybir.AxisListType.X, op=ALU.min
+    )
+    total = small.tile([P, CHANNELS], F32, name="total")
+    nc.vector.tensor_tensor(out=total[:], in0=top[:], in1=bottom[:], op=ALU.add)
+    neg_mid = small.tile([P, CHANNELS], F32, name="neg_mid")
+    nc.vector.tensor_scalar(out=neg_mid[:], in0=total[:], scalar1=-0.5, scalar2=None, op0=ALU.mult)
+    return neg_mid
+
+
+def by_word_half(ap):
+    return ap.rearrange("p (q u e) -> p u q e", u=2, e=2)
+
+
+def turn(nc, psum_tr, identity, rows):
+    banks = []
+    for pair in range(GROUP // PAIR):
+        turned = psum_tr.tile([P, 2, PAIR * P], F32, name="turned")
+        for member in range(PAIR):
+            for u in range(2):
+                nc.tensor.transpose(
+                    turned[:, u, P * member : P * (member + 1)],
+                    rows[:, PAIR * pair + member, u, :].bitcast(F32),
+                    identity[:],
+                )
+        banks.append(turned)
+    return banks
+
+
+def gather_words(nc, work, banks, func, label):
+    grouped = work.tile([P, GROUP // PAIR, PAIR * P * 4], BF16, name=label + "_grouped", align_bytes=64)
+    for pair in range(GROUP // PAIR):
+        nc.scalar.activation(
+            out=grouped[:, pair, :].rearrange("p (w u e) -> p w u e", u=2, e=2),
+            in_=banks[pair][:].bitcast(BF16).rearrange("p u (w e) -> p w u e", e=2),
+            func=func,
+        )
+    return grouped
+
+
+def quantise(nc, work, grouped, label):
+    codes = work.tile([P, GROUP * P], U32, name=label + "_codes", align_bytes=64)
+    plane = work.tile([P, GROUP * P], U8, name=label + "_plane", align_bytes=64)
+    nc.vector.quantize_mx(
+        out=codes[:].bitcast(FP8X4), scales=plane[:], in_=grouped[:].rearrange("p a n -> p (a n)")
+    )
+    return codes, plane
+
+
+def layer(nc, psum_acc, operand, member, w_codes, w_planes, channel, label):
+    codes, plane = operand
+    cells = slice(P * member, P * (member + 1))
+    acc = psum_acc.tile([P, K], F32, name=label)
+    nc.tensor.matmul_mx(
+        out=acc[:],
+        lhsT=codes[:, cells].bitcast(FP8X4),
+        lhsT_scale=plane[:, cells],
+        rhs=w_codes[:, channel, :].bitcast(FP8X4),
+        rhs_scale=w_planes[:, channel, :],
+        start=True,
+        stop=True,
+    )
+    return acc
+
+
+def tile_shapeletencoder_pa_e_kernel(tc, x, W0_words, W0_scales, b0, W1_words, W1_scales, b1, out):
+    nc = tc.nc
+    with ExitStack() as ctx:
+        const = ctx.enter_context(tc.tile_pool(name="const", bufs=1))
+        series_pool = ctx.enter_context(tc.tile_pool(name="series", bufs=SERIES))
+        tree = ctx.enter_context(tc.tile_pool(name="tree", bufs=2))
+        small = ctx.enter_context(tc.tile_pool(name="small", bufs=SERIES))
+        work = ctx.enter_context(tc.tile_pool(name="work", bufs=2))
+        results = ctx.enter_context(tc.tile_pool(name="results", bufs=3))
+        psum_tr = ctx.enter_context(tc.psum_pool(name="psum_tr", bufs=4))
+        psum_acc = ctx.enter_context(tc.psum_pool(name="psum_acc", bufs=2))
+        ctx.enter_context(tc.manual_schedule())
+
+        identity = const.tile([P, P], F32, name="identity")
+        make_identity(nc, identity[:])
+        w0_codes, w0_planes = load_weight(nc, const, "w0")
+        w1_codes, w1_planes = load_weight(nc, const, "w1")
+
+        x_tiles = []
+        for s in range(SERIES):
+            x_tiles.append(series_pool.tile([P, K * CHANNELS], BF16, name="x_tile"))
+
+        def load_series(s):
+            nc.sync.dma_start(out=x_tiles[s][:], in_=x[s].rearrange("(s l) c -> s (l c)", l=K))
+
+        load_series(0)
+        load_series(1)
+        load_scale_rows(nc, w0_planes, W0_scales)
+        load_scale_rows(nc, w1_planes, W1_scales)
+        load_codes(nc, w0_codes, W0_words, 0)
+        b0_spread = load_bias(nc, const, b0, "b0_spread")
+        load_series(2)
+        load_codes(nc, w0_codes, W0_words, GROUP)
+        load_codes(nc, w1_codes, W1_words, 0)
+        b1_spread = load_bias(nc, const, b1, "b1_spread")
+        load_codes(nc, w1_codes, W1_words, GROUP)
+        load_series(3)
+
+        groups = SERIES * CHANNELS // GROUP
+        per_series = CHANNELS // GROUP
+        neg_mid = {}
+        n_banks = {}
+        n_grouped = {}
+        h_rows = {}
+        h_grouped = {}
+
+        def midpoints(s):
+            if 0 <= s < SERIES:
+                neg_mid[s] = negative_midpoints(nc, tree, small, x_tiles[s])
+
+        def subtract_and_turn(g):
+            if not 0 <= g < groups:
+                return
+            s = g // per_series
+            first = GROUP * (g % per_series)
+            x_by_channel = x_tiles[s][:].rearrange("p (q u e c) -> p c u q e", u=2, e=2, c=CHANNELS)
+            n_rows = work.tile([P, GROUP, 2, K // 2], BF16, name="n_rows")
+            for member in range(GROUP):
+                channel = first + member
+                nc.scalar.activation(
+                    out=n_rows[:, member, :, :].rearrange("p u (q e) -> p u q e", e=2),
+                    in_=x_by_channel[:, channel],
+                    func=ACT.Identity,
+                    bias=neg_mid[s][:, channel : channel + 1],
+                    scale=1.0,
+                )
+            n_banks[g] = turn(nc, psum_tr, identity, n_rows)
+
+        def gather_n(g):
+            if 0 <= g < groups:
+                n_grouped[g] = gather_words(nc, work, n_banks[g], ACT.Copy, "n")
+
+        def first_layer(g, n_operand):
+            first = GROUP * (g % per_series)
+            h_rows[g] = work.tile([P, GROUP, 2, K // 2], BF16, name="h_rows")
+            for member in range(GROUP):
+                channel = first + member
+                acc0 = layer(nc, psum_acc, n_operand, member, w0_codes, w0_planes, channel, "acc0")
+                nc.vector.tensor_tensor(
+                    out=h_rows[g][:, member, :, :].rearrange("p u (q e) -> p u q e", e=2),
+                    in0=by_word_half(acc0[:]),
+                    in1=by_word_half(b0_spread[:, channel, :]),
+                    op=ALU.add,
+                )
+
+        def second_layer(g, h_operand):
+            s = g // per_series
+            first = GROUP * (g % per_series)
+            result = results.tile([P, GROUP, K], F32, name="result")
+            for member in range(GROUP):
+                channel = first + member
+                acc1 = layer(nc, psum_acc, h_operand, member, w1_codes, w1_planes, channel, "acc1")
+                nc.vector.tensor_tensor(
+                    out=result[:, member, :], in0=acc1[:], in1=b1_spread[:, channel, :], op=ALU.add
+                )
+                nc.gpsimd.tensor_scalar(
+                    out=result[:, member, :],
+                    in0=result[:, member, :],
+                    scalar1=FLT_MAX,
+                    scalar2=0.0,
+                    op0=ALU.min,
+                    op1=ALU.max,
+                )
+                if member % PAIR == PAIR - 1:
+                    done = slice(member + 1 - PAIR, member + 1)
+                    nc.sync.dma_start(
+                        out=out[s, :, first + member + 1 - PAIR : first + member + 1, :].rearrange("s c k -> s (c k)"),
+                        in_=result[:, done, :].rearrange("p c k -> p (c k)"),
+                    )
+
+        midpoints(0)
+        midpoints(1)
+        for i in range(-2, groups + 1):
+            n_operand = quantise(nc, work, n_grouped[i], "n") if 0 <= i < groups else None
+            h_operand = quantise(nc, work, h_grouped[i - 1], "h") if 0 <= i - 1 < groups else None
+            gather_n(i + 1)
+            if n_operand is not None:
+                first_layer(i, n_operand)
+            if h_operand is not None:
+                second_layer(i - 1, h_operand)
+            if 0 <= i < groups:
+                h_banks = turn(nc, psum_tr, identity, h_rows[i])
+            subtract_and_turn(i + 2)
+            if 0 <= i < groups:
+                h_grouped[i] = gather_words(nc, work, h_banks, ACT.Relu, "h")
+            if i >= 0 and i % per_series == 0:
+                midpoints(i // per_series + 2)

@@ -16,10 +16,11 @@ P = 128
 SERIES = 4
 CHANNELS = 8
 K = 512
-GROUP = 4
 PAIR = 2
+HALF = 4
 TREE_LEVELS = 4
-FLT_MAX = 3.4028234663852886e38
+UNITS = SERIES * CHANNELS // PAIR
+UNITS_PER_SERIES = CHANNELS // PAIR
 
 FLOPS = 2 * 2 * SERIES * P * CHANNELS * K * K
 
@@ -41,8 +42,8 @@ def load_scale_rows(nc, planes, scales):
 
 def load_codes(nc, codes, words, first):
     nc.sync.dma_start(
-        out=codes[:, first : first + GROUP, :].bitcast(I32),
-        in_=words[first : first + GROUP].rearrange("g p n t -> p g (n t)").bitcast(I32),
+        out=codes[:, first : first + HALF, :].bitcast(I32),
+        in_=words[first : first + HALF].rearrange("g p n t -> p g (n t)").bitcast(I32),
     )
 
 
@@ -55,35 +56,20 @@ def load_bias(nc, pool, bias, label):
     return spread
 
 
-def negative_midpoints(nc, tree, small, x_tile):
-    high = x_tile
-    low = x_tile
-    width = K * CHANNELS
-    for level in range(TREE_LEVELS):
-        width //= 2
-        high_next = tree.tile([P, width], BF16, name="high%d" % level)
-        low_next = tree.tile([P, width], BF16, name="low%d" % level)
-        nc.vector.tensor_tensor(
-            out=high_next[:], in0=high[:, 0:width], in1=high[:, width : 2 * width], op=ALU.max
-        )
-        nc.vector.tensor_tensor(
-            out=low_next[:], in0=low[:, 0:width], in1=low[:, width : 2 * width], op=ALU.min
-        )
-        high = high_next
-        low = low_next
-    top = small.tile([P, CHANNELS], F32, name="top")
-    bottom = small.tile([P, CHANNELS], F32, name="bottom")
-    nc.vector.tensor_reduce(
-        out=top[:], in_=high[:].rearrange("p (l c) -> p c l", c=CHANNELS), axis=mybir.AxisListType.X, op=ALU.max
-    )
-    nc.vector.tensor_reduce(
-        out=bottom[:], in_=low[:].rearrange("p (l c) -> p c l", c=CHANNELS), axis=mybir.AxisListType.X, op=ALU.min
-    )
-    total = small.tile([P, CHANNELS], F32, name="total")
-    nc.vector.tensor_tensor(out=total[:], in0=top[:], in1=bottom[:], op=ALU.add)
-    neg_mid = small.tile([P, CHANNELS], F32, name="neg_mid")
-    nc.vector.tensor_scalar(out=neg_mid[:], in0=total[:], scalar1=-0.5, scalar2=None, op0=ALU.mult)
-    return neg_mid
+def halve(nc, tree, high, low, width, level):
+    high_next = tree.tile([P, width], BF16, name="high%d" % level)
+    low_next = tree.tile([P, width], BF16, name="low%d" % level)
+    nc.vector.tensor_tensor(out=by_step(high_next[:]), in0=high[0], in1=high[1], op=ALU.max)
+    nc.vector.tensor_tensor(out=by_step(low_next[:]), in0=low[0], in1=low[1], op=ALU.min)
+    return high_next, low_next
+
+
+def by_step(ap):
+    return ap.rearrange("p (l c) -> p l c", c=HALF)
+
+
+def halves(tile_ap, width):
+    return by_step(tile_ap[:, 0:width]), by_step(tile_ap[:, width : 2 * width])
 
 
 def by_word_half(ap):
@@ -91,54 +77,49 @@ def by_word_half(ap):
 
 
 def turn(nc, psum_tr, identity, rows):
-    banks = []
-    for pair in range(GROUP // PAIR):
-        turned = psum_tr.tile([P, 2, PAIR * P], F32, name="turned")
-        for member in range(PAIR):
-            for u in range(2):
-                nc.tensor.transpose(
-                    turned[:, u, P * member : P * (member + 1)],
-                    rows[:, PAIR * pair + member, u, :].bitcast(F32),
-                    identity[:],
-                )
-        banks.append(turned)
-    return banks
+    turned = psum_tr.tile([P, 2, PAIR * P], F32, name="turned")
+    for member in range(PAIR):
+        for u in range(2):
+            nc.tensor.transpose(
+                turned[:, u, P * member : P * (member + 1)], rows[:, member, u, :].bitcast(F32), identity[:]
+            )
+    return turned
 
 
-def gather_words(nc, work, banks, func, label):
-    grouped = work.tile([P, GROUP // PAIR, PAIR * P * 4], BF16, name=label + "_grouped", align_bytes=64)
-    for pair in range(GROUP // PAIR):
-        nc.scalar.activation(
-            out=grouped[:, pair, :].rearrange("p (w u e) -> p w u e", u=2, e=2),
-            in_=banks[pair][:].bitcast(BF16).rearrange("p u (w e) -> p w u e", e=2),
-            func=func,
-        )
+def gather_words(nc, work, turned, func, label):
+    grouped = work.tile([P, PAIR * P * 4], BF16, name=label + "_grouped", align_bytes=64)
+    nc.scalar.activation(
+        out=grouped[:].rearrange("p (w u e) -> p w u e", u=2, e=2),
+        in_=turned[:].bitcast(BF16).rearrange("p u (w e) -> p w u e", e=2),
+        func=func,
+    )
     return grouped
 
 
 def quantise(nc, work, grouped, label):
-    codes = work.tile([P, GROUP * P], U32, name=label + "_codes", align_bytes=64)
-    plane = work.tile([P, GROUP * P], U8, name=label + "_plane", align_bytes=64)
-    nc.vector.quantize_mx(
-        out=codes[:].bitcast(FP8X4), scales=plane[:], in_=grouped[:].rearrange("p a n -> p (a n)")
-    )
+    codes = work.tile([P, PAIR * P], U32, name=label + "_codes", align_bytes=64)
+    plane = work.tile([P, PAIR * P], U8, name=label + "_plane", align_bytes=64)
+    nc.vector.quantize_mx(out=codes[:].bitcast(FP8X4), scales=plane[:], in_=grouped[:])
     return codes, plane
 
 
-def layer(nc, psum_acc, operand, member, w_codes, w_planes, channel, label):
+def multiply(nc, psum_acc, operand, w_codes, w_planes, first, label):
     codes, plane = operand
-    cells = slice(P * member, P * (member + 1))
-    acc = psum_acc.tile([P, K], F32, name=label)
-    nc.tensor.matmul_mx(
-        out=acc[:],
-        lhsT=codes[:, cells].bitcast(FP8X4),
-        lhsT_scale=plane[:, cells],
-        rhs=w_codes[:, channel, :].bitcast(FP8X4),
-        rhs_scale=w_planes[:, channel, :],
-        start=True,
-        stop=True,
-    )
-    return acc
+    sums = []
+    for member in range(PAIR):
+        cells = slice(P * member, P * (member + 1))
+        acc = psum_acc.tile([P, K], F32, name=label)
+        nc.tensor.matmul_mx(
+            out=acc[:],
+            lhsT=codes[:, cells].bitcast(FP8X4),
+            lhsT_scale=plane[:, cells],
+            rhs=w_codes[:, first + member, :].bitcast(FP8X4),
+            rhs_scale=w_planes[:, first + member, :],
+            start=True,
+            stop=True,
+        )
+        sums.append(acc)
+    return sums
 
 
 def tile_shapeletencoder_pa_e_kernel(tc, x, W0_words, W0_scales, b0, W1_words, W1_scales, b1, out):
@@ -147,9 +128,9 @@ def tile_shapeletencoder_pa_e_kernel(tc, x, W0_words, W0_scales, b0, W1_words, W
         const = ctx.enter_context(tc.tile_pool(name="const", bufs=1))
         series_pool = ctx.enter_context(tc.tile_pool(name="series", bufs=SERIES))
         tree = ctx.enter_context(tc.tile_pool(name="tree", bufs=2))
-        small = ctx.enter_context(tc.tile_pool(name="small", bufs=SERIES))
+        small = ctx.enter_context(tc.tile_pool(name="small", bufs=4))
         work = ctx.enter_context(tc.tile_pool(name="work", bufs=2))
-        results = ctx.enter_context(tc.tile_pool(name="results", bufs=3))
+        results = ctx.enter_context(tc.tile_pool(name="results", bufs=4))
         psum_tr = ctx.enter_context(tc.psum_pool(name="psum_tr", bufs=4))
         psum_acc = ctx.enter_context(tc.psum_pool(name="psum_acc", bufs=2))
         ctx.enter_context(tc.manual_schedule())
@@ -169,102 +150,121 @@ def tile_shapeletencoder_pa_e_kernel(tc, x, W0_words, W0_scales, b0, W1_words, W
         load_series(0)
         load_series(1)
         load_scale_rows(nc, w0_planes, W0_scales)
-        load_scale_rows(nc, w1_planes, W1_scales)
         load_codes(nc, w0_codes, W0_words, 0)
         b0_spread = load_bias(nc, const, b0, "b0_spread")
-        load_series(2)
-        load_codes(nc, w0_codes, W0_words, GROUP)
+        load_codes(nc, w0_codes, W0_words, HALF)
+        load_scale_rows(nc, w1_planes, W1_scales)
         load_codes(nc, w1_codes, W1_words, 0)
         b1_spread = load_bias(nc, const, b1, "b1_spread")
-        load_codes(nc, w1_codes, W1_words, GROUP)
+        load_series(2)
+        load_codes(nc, w1_codes, W1_words, HALF)
         load_series(3)
 
-        groups = SERIES * CHANNELS // GROUP
-        per_series = CHANNELS // GROUP
+        tree_top = {}
         neg_mid = {}
-        n_banks = {}
+        n_turned = {}
         n_grouped = {}
+        n_operand = {}
+        sums0 = {}
         h_rows = {}
+        h_turned = {}
         h_grouped = {}
+        h_operand = {}
+        sums1 = {}
 
-        def midpoints(s):
-            if 0 <= s < SERIES:
-                neg_mid[s] = negative_midpoints(nc, tree, small, x_tiles[s])
+        def is_unit(j):
+            return 0 <= j < UNITS
 
-        def subtract_and_turn(g):
-            if not 0 <= g < groups:
-                return
-            s = g // per_series
-            first = GROUP * (g % per_series)
-            x_by_channel = x_tiles[s][:].rearrange("p (q u e c) -> p c u q e", u=2, e=2, c=CHANNELS)
-            n_rows = work.tile([P, GROUP, 2, K // 2], BF16, name="n_rows")
-            for member in range(GROUP):
-                channel = first + member
+        def first_channel(j):
+            return PAIR * (j % UNITS_PER_SERIES)
+
+        def start_trees(t):
+            steps = x_tiles[t // 2][:].rearrange("p (l c) -> p l c", c=CHANNELS)
+            mine = steps[:, :, HALF * (t % 2) : HALF * (t % 2) + HALF]
+            pair_of_halves = (mine[:, 0 : K // 2, :], mine[:, K // 2 : K, :])
+            tree_top[t] = halve(nc, tree, pair_of_halves, pair_of_halves, HALF * K // 2, 0)
+
+        def finish_trees(t):
+            high, low = tree_top[t]
+            width = HALF * K // 2
+            for level in range(1, TREE_LEVELS):
+                width //= 2
+                high, low = halve(nc, tree, halves(high, width), halves(low, width), width, level)
+            top = small.tile([P, HALF], F32, name="top")
+            bottom = small.tile([P, HALF], F32, name="bottom")
+            nc.vector.tensor_reduce(
+                out=top[:], in_=high[:].rearrange("p (l c) -> p c l", c=HALF), axis=mybir.AxisListType.X, op=ALU.max
+            )
+            nc.vector.tensor_reduce(
+                out=bottom[:], in_=low[:].rearrange("p (l c) -> p c l", c=HALF), axis=mybir.AxisListType.X, op=ALU.min
+            )
+            total = small.tile([P, HALF], F32, name="total")
+            nc.vector.tensor_tensor(out=total[:], in0=top[:], in1=bottom[:], op=ALU.add)
+            neg_mid[t] = small.tile([P, HALF], F32, name="neg_mid")
+            nc.vector.tensor_scalar(out=neg_mid[t][:], in0=total[:], scalar1=-0.5, scalar2=None, op0=ALU.mult)
+
+        def subtract_and_turn(j):
+            x_by_channel = x_tiles[j // UNITS_PER_SERIES][:].rearrange(
+                "p (q u e c) -> p c u q e", u=2, e=2, c=CHANNELS
+            )
+            n_rows = work.tile([P, PAIR, 2, K // 2], BF16, name="n_rows")
+            for member in range(PAIR):
+                channel = first_channel(j) + member
                 nc.scalar.activation(
                     out=n_rows[:, member, :, :].rearrange("p u (q e) -> p u q e", e=2),
                     in_=x_by_channel[:, channel],
                     func=ACT.Identity,
-                    bias=neg_mid[s][:, channel : channel + 1],
+                    bias=neg_mid[PAIR * j // HALF][:, channel % HALF : channel % HALF + 1],
                     scale=1.0,
                 )
-            n_banks[g] = turn(nc, psum_tr, identity, n_rows)
+            n_turned[j] = turn(nc, psum_tr, identity, n_rows)
 
-        def gather_n(g):
-            if 0 <= g < groups:
-                n_grouped[g] = gather_words(nc, work, n_banks[g], ACT.Copy, "n")
-
-        def first_layer(g, n_operand):
-            first = GROUP * (g % per_series)
-            h_rows[g] = work.tile([P, GROUP, 2, K // 2], BF16, name="h_rows")
-            for member in range(GROUP):
-                channel = first + member
-                acc0 = layer(nc, psum_acc, n_operand, member, w0_codes, w0_planes, channel, "acc0")
+        def add_first_bias(j):
+            h_rows[j] = work.tile([P, PAIR, 2, K // 2], BF16, name="h_rows")
+            for member in range(PAIR):
                 nc.vector.tensor_tensor(
-                    out=h_rows[g][:, member, :, :].rearrange("p u (q e) -> p u q e", e=2),
-                    in0=by_word_half(acc0[:]),
-                    in1=by_word_half(b0_spread[:, channel, :]),
+                    out=h_rows[j][:, member, :, :].rearrange("p u (q e) -> p u q e", e=2),
+                    in0=by_word_half(sums0[j][member][:]),
+                    in1=by_word_half(b0_spread[:, first_channel(j) + member, :]),
                     op=ALU.add,
                 )
 
-        def second_layer(g, h_operand):
-            s = g // per_series
-            first = GROUP * (g % per_series)
-            result = results.tile([P, GROUP, K], F32, name="result")
-            for member in range(GROUP):
-                channel = first + member
-                acc1 = layer(nc, psum_acc, h_operand, member, w1_codes, w1_planes, channel, "acc1")
+        def finish(j):
+            first = first_channel(j)
+            result = results.tile([P, PAIR, K], F32, name="result")
+            for member in range(PAIR):
                 nc.vector.tensor_tensor(
-                    out=result[:, member, :], in0=acc1[:], in1=b1_spread[:, channel, :], op=ALU.add
+                    out=result[:, member, :], in0=sums1[j][member][:], in1=b1_spread[:, first + member, :], op=ALU.add
                 )
-                nc.gpsimd.tensor_scalar(
-                    out=result[:, member, :],
-                    in0=result[:, member, :],
-                    scalar1=FLT_MAX,
-                    scalar2=0.0,
-                    op0=ALU.min,
-                    op1=ALU.max,
-                )
-                if member % PAIR == PAIR - 1:
-                    done = slice(member + 1 - PAIR, member + 1)
-                    nc.sync.dma_start(
-                        out=out[s, :, first + member + 1 - PAIR : first + member + 1, :].rearrange("s c k -> s (c k)"),
-                        in_=result[:, done, :].rearrange("p c k -> p (c k)"),
-                    )
+            flat = result[:].rearrange("p c k -> p (c k)")
+            nc.vector.tensor_scalar(out=flat, in0=flat, scalar1=0.0, scalar2=None, op0=ALU.max)
+            nc.sync.dma_start(
+                out=out[j // UNITS_PER_SERIES, :, first : first + PAIR, :].rearrange("s c k -> s (c k)"), in_=flat
+            )
 
-        midpoints(0)
-        midpoints(1)
-        for i in range(-2, groups + 1):
-            n_operand = quantise(nc, work, n_grouped[i], "n") if 0 <= i < groups else None
-            h_operand = quantise(nc, work, h_grouped[i - 1], "h") if 0 <= i - 1 < groups else None
-            gather_n(i + 1)
-            if n_operand is not None:
-                first_layer(i, n_operand)
-            if h_operand is not None:
-                second_layer(i - 1, h_operand)
-            if 0 <= i < groups:
-                h_banks = turn(nc, psum_tr, identity, h_rows[i])
-            subtract_and_turn(i + 2)
-            if 0 <= i < groups:
-                h_grouped[i] = gather_words(nc, work, h_banks, ACT.Relu, "h")
-            if i >= 0 and i % per_series == 0:
-                midpoints(i // per_series + 2)
+        for i in range(-6, UNITS + 1):
+            if is_unit(i - 1):
+                sums1[i - 1] = multiply(nc, psum_acc, h_operand[i - 1], w1_codes, w1_planes, first_channel(i - 1), "acc1")
+            if is_unit(i):
+                add_first_bias(i)
+            if is_unit(i + 1):
+                n_operand[i + 1] = quantise(nc, work, n_grouped[i + 1], "n")
+            if is_unit(i - 1):
+                finish(i - 1)
+            if is_unit(i):
+                h_turned[i] = turn(nc, psum_tr, identity, h_rows[i])
+            if is_unit(i + 3):
+                subtract_and_turn(i + 3)
+            if is_unit(i + 1):
+                sums0[i + 1] = multiply(nc, psum_acc, n_operand[i + 1], w0_codes, w0_planes, first_channel(i + 1), "acc0")
+            if is_unit(i + 2):
+                n_grouped[i + 2] = gather_words(nc, work, n_turned[i + 2], ACT.Copy, "n")
+            if is_unit(i):
+                h_grouped[i] = gather_words(nc, work, h_turned[i], ACT.Relu, "h")
+            if (i + 6) // 2 < 2 * SERIES:
+                if (i + 6) % 2 == 0:
+                    start_trees((i + 6) // 2)
+                else:
+                    finish_trees((i + 6) // 2)
+            if is_unit(i):
+                h_operand[i] = quantise(nc, work, h_grouped[i], "h")

@@ -128,12 +128,12 @@ def tile_shapeletencoder_pa_e_kernel(tc, x, W0_words, W0_scales, b0, W1_words, W
         const = ctx.enter_context(tc.tile_pool(name="const", bufs=1))
         series_pool = ctx.enter_context(tc.tile_pool(name="series", bufs=SERIES))
         tree = ctx.enter_context(tc.tile_pool(name="tree", bufs=2))
-        small = ctx.enter_context(tc.tile_pool(name="small", bufs=4))
-        work = ctx.enter_context(tc.tile_pool(name="work", bufs=2))
+        small = ctx.enter_context(tc.tile_pool(name="small", bufs=2 * SERIES))
+        work = ctx.enter_context(tc.tile_pool(name="work", bufs=4))
+        ahead = ctx.enter_context(tc.tile_pool(name="ahead", bufs=8))
         results = ctx.enter_context(tc.tile_pool(name="results", bufs=4))
         psum_tr = ctx.enter_context(tc.psum_pool(name="psum_tr", bufs=4))
         psum_acc = ctx.enter_context(tc.psum_pool(name="psum_acc", bufs=2))
-        ctx.enter_context(tc.manual_schedule())
 
         identity = const.tile([P, P], F32, name="identity")
         make_identity(nc, identity[:])
@@ -147,8 +147,8 @@ def tile_shapeletencoder_pa_e_kernel(tc, x, W0_words, W0_scales, b0, W1_words, W
         def load_series(s):
             nc.sync.dma_start(out=x_tiles[s][:], in_=x[s].rearrange("(s l) c -> s (l c)", l=K))
 
-        load_series(0)
-        load_series(1)
+        for s in range(SERIES):
+            load_series(s)
         load_scale_rows(nc, w0_planes, W0_scales)
         load_codes(nc, w0_codes, W0_words, 0)
         b0_spread = load_bias(nc, const, b0, "b0_spread")
@@ -156,9 +156,7 @@ def tile_shapeletencoder_pa_e_kernel(tc, x, W0_words, W0_scales, b0, W1_words, W
         load_scale_rows(nc, w1_planes, W1_scales)
         load_codes(nc, w1_codes, W1_words, 0)
         b1_spread = load_bias(nc, const, b1, "b1_spread")
-        load_series(2)
         load_codes(nc, w1_codes, W1_words, HALF)
-        load_series(3)
 
         tree_top = {}
         neg_mid = {}
@@ -237,12 +235,16 @@ def tile_shapeletencoder_pa_e_kernel(tc, x, W0_words, W0_scales, b0, W1_words, W
                     out=result[:, member, :], in0=sums1[j][member][:], in1=b1_spread[:, first + member, :], op=ALU.add
                 )
             flat = result[:].rearrange("p c k -> p (c k)")
-            nc.vector.tensor_scalar(out=flat, in0=flat, scalar1=0.0, scalar2=None, op0=ALU.max)
+            nc.any.tensor_relu(out=flat, in_=flat)
             nc.sync.dma_start(
                 out=out[j // UNITS_PER_SERIES, :, first : first + PAIR, :].rearrange("s c k -> s (c k)"), in_=flat
             )
 
-        for i in range(-6, UNITS + 1):
+        for t in range(2 * SERIES):
+            start_trees(t)
+            finish_trees(t)
+
+        for i in range(-3, UNITS + 1):
             if is_unit(i - 1):
                 sums1[i - 1] = multiply(nc, psum_acc, h_operand[i - 1], w1_codes, w1_planes, first_channel(i - 1), "acc1")
             if is_unit(i):
@@ -258,13 +260,8 @@ def tile_shapeletencoder_pa_e_kernel(tc, x, W0_words, W0_scales, b0, W1_words, W
             if is_unit(i + 1):
                 sums0[i + 1] = multiply(nc, psum_acc, n_operand[i + 1], w0_codes, w0_planes, first_channel(i + 1), "acc0")
             if is_unit(i + 2):
-                n_grouped[i + 2] = gather_words(nc, work, n_turned[i + 2], ACT.Copy, "n")
+                n_grouped[i + 2] = gather_words(nc, ahead, n_turned[i + 2], ACT.Copy, "n")
             if is_unit(i):
                 h_grouped[i] = gather_words(nc, work, h_turned[i], ACT.Relu, "h")
-            if (i + 6) // 2 < 2 * SERIES:
-                if (i + 6) % 2 == 0:
-                    start_trees((i + 6) // 2)
-                else:
-                    finish_trees((i + 6) // 2)
             if is_unit(i):
                 h_operand[i] = quantise(nc, work, h_grouped[i], "h")

@@ -16,28 +16,27 @@ P = 128
 SERIES = 4
 CHANNELS = 8
 K = 512
-PAIR = 2
+PACK = 4
 HALF = 4
 TREE_LEVELS = 4
-UNITS = SERIES * CHANNELS // PAIR
-UNITS_PER_SERIES = CHANNELS // PAIR
+
+RUNS = ((0, 1, 0), (1, 1, 0), (0, 2, 1), (2, 2, 0), (2, 2, 1))
+UNITS = HALF * len(RUNS)
+BLOCKS = UNITS // 2
 
 FLOPS = 2 * 2 * SERIES * P * CHANNELS * K * K
 
 
-def load_weight(nc, pool, label):
-    codes = pool.tile([P, CHANNELS, K], U32, name=label + "_codes", align_bytes=64)
-    planes = pool.tile([P, CHANNELS, K], U8, name=label + "_planes", align_bytes=64)
+def load_planes(nc, pool, scales, label):
+    planes = pool.tile([P, CHANNELS // HALF, K], U8, name=label + "_planes", align_bytes=64)
     nc.vector.memset(planes[:].bitcast(I32), 0)
-    return codes, planes
-
-
-def load_scale_rows(nc, planes, scales):
-    for quadrant in range(4):
-        nc.sync.dma_start(
-            out=planes[32 * quadrant : 32 * quadrant + 4, :, :].bitcast(I32),
-            in_=scales[:, 4 * quadrant : 4 * quadrant + 4, :].rearrange("g q n -> q g n").bitcast(I32),
-        )
+    for h in range(CHANNELS // HALF):
+        for quadrant in range(4):
+            nc.sync.dma_start(
+                out=planes[32 * quadrant : 32 * quadrant + 4 * HALF, h, :].bitcast(I32),
+                in_=scales[HALF * h : HALF * h + HALF, 4 * quadrant : 4 * quadrant + 4, :].bitcast(I32),
+            )
+    return planes
 
 
 def load_codes(nc, codes, words, first):
@@ -45,15 +44,6 @@ def load_codes(nc, codes, words, first):
         out=codes[:, first : first + HALF, :].bitcast(I32),
         in_=words[first : first + HALF].rearrange("g p n t -> p g (n t)").bitcast(I32),
     )
-
-
-def load_bias(nc, pool, bias, label):
-    spread = pool.tile([P, CHANNELS, K], BF16, name=label)
-    nc.sync.dma_start(
-        out=spread[:].rearrange("p c k -> p (c k)"),
-        in_=bias.rearrange("c k -> (c k)").partition_broadcast(P),
-    )
-    return spread
 
 
 def halve(nc, tree, high, low, width, level):
@@ -72,56 +62,6 @@ def halves(tile_ap, width):
     return by_step(tile_ap[:, 0:width]), by_step(tile_ap[:, width : 2 * width])
 
 
-def by_word_half(ap):
-    return ap.rearrange("p (q u e) -> p u q e", u=2, e=2)
-
-
-def turn(nc, psum_tr, identity, rows):
-    turned = psum_tr.tile([P, 2, PAIR * P], F32, name="turned")
-    for member in range(PAIR):
-        for u in range(2):
-            nc.tensor.transpose(
-                turned[:, u, P * member : P * (member + 1)], rows[:, member, u, :].bitcast(F32), identity[:]
-            )
-    return turned
-
-
-def gather_words(nc, work, turned, func, label):
-    grouped = work.tile([P, PAIR * P * 4], BF16, name=label + "_grouped", align_bytes=64)
-    nc.scalar.activation(
-        out=grouped[:].rearrange("p (w u e) -> p w u e", u=2, e=2),
-        in_=turned[:].bitcast(BF16).rearrange("p u (w e) -> p w u e", e=2),
-        func=func,
-    )
-    return grouped
-
-
-def quantise(nc, work, grouped, label):
-    codes = work.tile([P, PAIR * P], U32, name=label + "_codes", align_bytes=64)
-    plane = work.tile([P, PAIR * P], U8, name=label + "_plane", align_bytes=64)
-    nc.vector.quantize_mx(out=codes[:].bitcast(FP8X4), scales=plane[:], in_=grouped[:])
-    return codes, plane
-
-
-def multiply(nc, psum_acc, operand, w_codes, w_planes, first, label):
-    codes, plane = operand
-    sums = []
-    for member in range(PAIR):
-        cells = slice(P * member, P * (member + 1))
-        acc = psum_acc.tile([P, K], F32, name=label)
-        nc.tensor.matmul_mx(
-            out=acc[:],
-            lhsT=codes[:, cells].bitcast(FP8X4),
-            lhsT_scale=plane[:, cells],
-            rhs=w_codes[:, first + member, :].bitcast(FP8X4),
-            rhs_scale=w_planes[:, first + member, :],
-            start=True,
-            stop=True,
-        )
-        sums.append(acc)
-    return sums
-
-
 def tile_shapeletencoder_pa_e_kernel(tc, x, W0_words, W0_scales, b0, W1_words, W1_scales, b1, out):
     nc = tc.nc
     with ExitStack() as ctx:
@@ -129,61 +69,81 @@ def tile_shapeletencoder_pa_e_kernel(tc, x, W0_words, W0_scales, b0, W1_words, W
         series_pool = ctx.enter_context(tc.tile_pool(name="series", bufs=SERIES))
         tree = ctx.enter_context(tc.tile_pool(name="tree", bufs=2))
         small = ctx.enter_context(tc.tile_pool(name="small", bufs=2 * SERIES))
-        work = ctx.enter_context(tc.tile_pool(name="work", bufs=4))
-        ahead = ctx.enter_context(tc.tile_pool(name="ahead", bufs=8))
+        work = ctx.enter_context(tc.tile_pool(name="work", bufs=5))
         results = ctx.enter_context(tc.tile_pool(name="results", bufs=4))
-        psum_tr = ctx.enter_context(tc.psum_pool(name="psum_tr", bufs=4))
+        psum_xt = ctx.enter_context(tc.psum_pool(name="psum_xt", bufs=2))
         psum_acc = ctx.enter_context(tc.psum_pool(name="psum_acc", bufs=2))
+        psum_out = ctx.enter_context(tc.psum_pool(name="psum_out", bufs=2))
 
         identity = const.tile([P, P], F32, name="identity")
         make_identity(nc, identity[:])
-        w0_codes, w0_planes = load_weight(nc, const, "w0")
-        w1_codes, w1_planes = load_weight(nc, const, "w1")
+
+        w0_raw = const.tile([P, CHANNELS, K], U32, name="w0_raw", align_bytes=64)
+        w0_codes = const.tile([P, CHANNELS, K], U32, name="w0_codes", align_bytes=64)
+        w1_codes = const.tile([P, CHANNELS, K], U32, name="w1_codes", align_bytes=64)
+        w0_planes = const.tile([P, CHANNELS // HALF, K], U8, name="w0_planes", align_bytes=64)
+        b0_columns = const.tile([P, CHANNELS, PACK], BF16, name="b0_columns")
+        b1_rows = const.tile([P, P], BF16, name="b1_rows")
+        nc.vector.memset(b1_rows[:], 0.0)
 
         x_tiles = []
         for s in range(SERIES):
             x_tiles.append(series_pool.tile([P, K * CHANNELS], BF16, name="x_tile"))
 
-        def load_series(s):
-            nc.sync.dma_start(out=x_tiles[s][:], in_=x[s].rearrange("(s l) c -> s (l c)", l=K))
+        def load_series(s, pieces):
+            width = K * CHANNELS // pieces
+            cells = x[s].rearrange("(s l) c -> s (l c)", l=K)
+            for piece in range(pieces):
+                columns = slice(width * piece, width * (piece + 1))
+                nc.sync.dma_start(out=x_tiles[s][:, columns], in_=cells[:, columns])
 
-        for s in range(SERIES):
-            load_series(s)
-        load_scale_rows(nc, w0_planes, W0_scales)
-        load_codes(nc, w0_codes, W0_words, 0)
-        b0_spread = load_bias(nc, const, b0, "b0_spread")
-        load_codes(nc, w0_codes, W0_words, HALF)
-        load_scale_rows(nc, w1_planes, W1_scales)
+        load_series(0, 2)
+        w0_raw_planes = load_planes(nc, const, W0_scales, "w0_raw")
+        load_codes(nc, w0_raw, W0_words, 0)
+        load_series(1, 1)
+        nc.sync.dma_start(out=b0_columns[:], in_=b0.rearrange("c (p t) -> p c t", t=PACK))
+        nc.sync.dma_start(out=b1_rows[0 : CHANNELS * PACK, :], in_=b1.rearrange("c (j p) -> (c j) p", p=P))
+        w1_planes = load_planes(nc, const, W1_scales, "w1")
         load_codes(nc, w1_codes, W1_words, 0)
-        b1_spread = load_bias(nc, const, b1, "b1_spread")
+        load_codes(nc, w0_raw, W0_words, HALF)
+        load_series(2, 1)
+        load_series(3, 1)
         load_codes(nc, w1_codes, W1_words, HALF)
 
         tree_top = {}
         neg_mid = {}
-        n_turned = {}
+        mid_rows = {}
+        b1_columns = const.tile([P, CHANNELS, PACK], F32, name="b1_columns")
+        xt = {}
         n_grouped = {}
         n_operand = {}
         sums0 = {}
         h_rows = {}
-        h_turned = {}
         h_grouped = {}
         h_operand = {}
         sums1 = {}
+        features = {}
+        turned_out = {}
 
-        def is_unit(j):
-            return 0 <= j < UNITS
+        def start_trees(s, half):
+            steps = x_tiles[s][:].rearrange("p (l c) -> p l c", c=CHANNELS)
+            mine = steps[:, :, HALF * half : HALF * half + HALF]
+            if s > 0:
+                pair_of_halves = (mine[:, 0 : K // 2, :], mine[:, K // 2 : K, :])
+                tree_top[s, half] = halve(nc, tree, pair_of_halves, pair_of_halves, HALF * K // 2, 0)
+                return
+            tree_top[s, half] = (
+                tree.tile([P, HALF * K // 2], BF16, name="high0"),
+                tree.tile([P, HALF * K // 2], BF16, name="low0"),
+            )
+            for part in range(2):
+                quarters = [mine[:, K // 4 * q : K // 4 * (q + 1), :] for q in (2 * part, 2 * part + 1)]
+                columns = slice(HALF * K // 4 * part, HALF * K // 4 * (part + 1))
+                for tops, op in zip(tree_top[s, half], (ALU.max, ALU.min)):
+                    nc.vector.tensor_tensor(out=by_step(tops[:, columns]), in0=quarters[0], in1=quarters[1], op=op)
 
-        def first_channel(j):
-            return PAIR * (j % UNITS_PER_SERIES)
-
-        def start_trees(t):
-            steps = x_tiles[t // 2][:].rearrange("p (l c) -> p l c", c=CHANNELS)
-            mine = steps[:, :, HALF * (t % 2) : HALF * (t % 2) + HALF]
-            pair_of_halves = (mine[:, 0 : K // 2, :], mine[:, K // 2 : K, :])
-            tree_top[t] = halve(nc, tree, pair_of_halves, pair_of_halves, HALF * K // 2, 0)
-
-        def finish_trees(t):
-            high, low = tree_top[t]
+        def finish_trees(s, half):
+            high, low = tree_top[s, half]
             width = HALF * K // 2
             for level in range(1, TREE_LEVELS):
                 width //= 2
@@ -198,70 +158,212 @@ def tile_shapeletencoder_pa_e_kernel(tc, x, W0_words, W0_scales, b0, W1_words, W
             )
             total = small.tile([P, HALF], F32, name="total")
             nc.vector.tensor_tensor(out=total[:], in0=top[:], in1=bottom[:], op=ALU.add)
-            neg_mid[t] = small.tile([P, HALF], F32, name="neg_mid")
-            nc.vector.tensor_scalar(out=neg_mid[t][:], in0=total[:], scalar1=-0.5, scalar2=None, op0=ALU.mult)
+            neg_mid[s, half] = small.tile([P, HALF], F32, name="neg_mid")
+            nc.vector.tensor_scalar(out=neg_mid[s, half][:], in0=total[:], scalar1=-0.5, scalar2=None, op0=ALU.mult)
 
-        def subtract_and_turn(j):
-            x_by_channel = x_tiles[j // UNITS_PER_SERIES][:].rearrange(
-                "p (q u e c) -> p c u q e", u=2, e=2, c=CHANNELS
+        def spread_midpoints(s, half):
+            spread = psum_xt.tile([P, HALF, P], F32, name="turned")
+            for c in range(HALF):
+                nc.tensor.transpose(spread[:, c, :], neg_mid[s, half][:, c : c + 1].to_broadcast([P, P]), identity[:])
+            rows = small.tile([P, HALF, P], F32, name="mid_rows")
+            nc.scalar.copy(out=rows[:], in_=spread[:])
+            mid_rows[s, half] = rows
+
+        def permute_first_weight(first, count):
+            nc.vector.tensor_copy(
+                out=w0_codes[:, first : first + count, :].bitcast(I32).rearrange("p c (t m) -> p c t m", t=PACK),
+                in_=w0_raw[:, first : first + count, :].bitcast(I32).rearrange("p c (m t) -> p c t m", t=PACK),
             )
-            n_rows = work.tile([P, PAIR, 2, K // 2], BF16, name="n_rows")
-            for member in range(PAIR):
-                channel = first_channel(j) + member
-                nc.scalar.activation(
-                    out=n_rows[:, member, :, :].rearrange("p u (q e) -> p u q e", e=2),
-                    in_=x_by_channel[:, channel],
-                    func=ACT.Identity,
-                    bias=neg_mid[PAIR * j // HALF][:, channel % HALF : channel % HALF + 1],
-                    scale=1.0,
-                )
-            n_turned[j] = turn(nc, psum_tr, identity, n_rows)
 
-        def add_first_bias(j):
-            h_rows[j] = work.tile([P, PAIR, 2, K // 2], BF16, name="h_rows")
-            for member in range(PAIR):
+        def permute_first_scales():
+            nc.vector.tensor_copy(
+                out=w0_planes[:].rearrange("p h (t m) -> p h t m", t=PACK),
+                in_=w0_raw_planes[:].rearrange("p h (m t) -> p h t m", t=PACK),
+            )
+
+        def turn_bias():
+            b1_wide = const.tile([P, P], F32, name="b1_wide")
+            nc.scalar.copy(out=b1_wide[:], in_=b1_rows[:])
+            b1_turned = psum_xt.tile([P, P], F32, name="turned")
+            nc.tensor.transpose(b1_turned[:], b1_wide[:], identity[:])
+            nc.scalar.copy(out=b1_columns[:].rearrange("p c j -> p (c j)"), in_=b1_turned[:, 0 : CHANNELS * PACK])
+
+        def is_unit(u):
+            return 0 <= u < UNITS
+
+        def series_of(u):
+            first, count, half = RUNS[u // HALF]
+            return range(first, first + count)
+
+        def channel_of(u):
+            return HALF * RUNS[u // HALF][2] + u % HALF
+
+        def series_of_turn(u):
+            return series_of(u)[u % 2 : u % 2 + 1]
+
+        def turn_steps(u):
+            pair = channel_of(u) // 2
+            for s in series_of_turn(u):
+                words = x_tiles[s][:].bitcast(F32).rearrange("p (q t c) -> p t c q", t=PACK, c=CHANNELS // 2)
+                xt[u] = psum_xt.tile([P, PACK, P], F32, name="turned")
+                for t in range(PACK):
+                    nc.tensor.transpose(xt[u][:, t, :], words[:, t, pair, :], identity[:])
+
+        def subtract(u):
+            half, first = divmod(channel_of(u - u % 2), HALF)
+            if u % 2 == 0:
+                n_grouped[u // 2] = work.tile([P, 2, len(series_of(u)), P, PACK], BF16, name="n_grouped", align_bytes=64)
+            for s in series_of_turn(u):
                 nc.vector.tensor_tensor(
-                    out=h_rows[j][:, member, :, :].rearrange("p u (q e) -> p u q e", e=2),
-                    in0=by_word_half(sums0[j][member][:]),
-                    in1=by_word_half(b0_spread[:, first_channel(j) + member, :]),
+                    out=n_grouped[u // 2][:, :, u % 2, :, :],
+                    in0=xt[u][:].bitcast(BF16).rearrange("p t (w e) -> p e w t", e=2),
+                    in1=mid_rows[s, half][:, first : first + 2, :].unsqueeze(3).to_broadcast([P, 2, P, PACK]),
                     op=ALU.add,
                 )
 
-        def finish(j):
-            first = first_channel(j)
-            result = results.tile([P, PAIR, K], F32, name="result")
-            for member in range(PAIR):
-                nc.vector.tensor_tensor(
-                    out=result[:, member, :], in0=sums1[j][member][:], in1=b1_spread[:, first + member, :], op=ALU.add
-                )
-            flat = result[:].rearrange("p c k -> p (c k)")
-            nc.any.tensor_relu(out=flat, in_=flat)
+        def quantise(grouped_flat, columns, label):
+            codes = work.tile([P, columns], U32, name=label + "_codes", align_bytes=64)
+            plane = work.tile([P, columns], U8, name=label + "_plane", align_bytes=64)
+            nc.vector.quantize_mx(out=codes[:].bitcast(FP8X4), scales=plane[:], in_=grouped_flat)
+            return codes, plane
+
+        def multiply(weight_codes, weight_planes, channel, codes, plane, label):
+            cells = codes.shape[1]
+            fit = K // cells
+            sums = []
+            for first in range(0, PACK, fit):
+                bank = psum_acc.tile([P, fit, cells], F32, name=label)
+                for side in range(fit):
+                    columns = slice(P * (first + side), P * (first + side + 1))
+                    sums.append(bank[:, side, :])
+                    nc.tensor.matmul_mx(
+                        out=bank[:, side, :],
+                        lhsT=weight_codes[:, channel, columns].bitcast(FP8X4),
+                        lhsT_scale=weight_planes[4 * (channel % HALF) : P, channel // HALF, columns],
+                        rhs=codes.bitcast(FP8X4),
+                        rhs_scale=plane,
+                        start=True,
+                        stop=True,
+                    )
+            return sums
+
+        def relu_with_bias(to, sums, column, on_vector):
+            if on_vector:
+                nc.vector.tensor_scalar(out=to, in0=sums, scalar1=column, scalar2=0.0, op0=ALU.add, op1=ALU.max)
+            else:
+                nc.scalar.activation(out=to, in_=sums, func=ACT.Relu, bias=column, scale=1.0)
+
+        def first_layer(u):
+            channel = channel_of(u)
+            codes, plane = n_operand[u]
+            sums0[u] = multiply(w0_codes, w0_planes, channel, codes[:], plane[:], "acc0")
+
+        def finish_first(u):
+            channel = channel_of(u)
+            h_rows[u] = work.tile([P, PACK, P * len(series_of(u))], BF16, name="h_rows")
+            for t in range(PACK):
+                relu_with_bias(h_rows[u][:, t, :], sums0[u][t], b0_columns[:, channel, t : t + 1], t < sums_on_vector(u))
+
+        def interleave(u):
+            h_grouped[u] = work.tile([P, P * len(series_of(u)), PACK], BF16, name="h_grouped", align_bytes=64)
+            nc.vector.tensor_copy(out=h_grouped[u][:], in_=h_rows[u][:].rearrange("p t n -> p n t"))
+
+        def second_layer(u):
+            channel = channel_of(u)
+            codes, plane = h_operand[u]
+            sums1[u] = multiply(w1_codes, w1_planes, channel, codes[:], plane[:], "acc1")
+
+        def finish_second(u):
+            channel = channel_of(u)
+            features[u] = work.tile([P, PACK, P * len(series_of(u))], F32, name="features")
+            for j in range(PACK):
+                relu_with_bias(features[u][:, j, :], sums1[u][j], b1_columns[:, channel, j : j + 1], j < sums_on_vector(u))
+
+        def turn_back(u):
+            turned_out[u] = []
+            for member in range(len(series_of(u))):
+                bank = psum_out.tile([P, K], F32, name="turned_out")
+                for j in range(PACK):
+                    nc.tensor.transpose(
+                        bank[:, P * j : P * (j + 1)], features[u][:, j, P * member : P * (member + 1)], identity[:]
+                    )
+                turned_out[u].append(bank)
+
+        def store(u):
+            channel = channel_of(u)
+            series = series_of(u)
+            result = results.tile([P, len(series), K], F32, name="result")
+            for member in range(len(series)):
+                if member >= copies_on_scalar(u):
+                    nc.vector.tensor_copy(out=result[:, member, :], in_=turned_out[u][member][:])
+                else:
+                    nc.scalar.copy(out=result[:, member, :], in_=turned_out[u][member][:])
             nc.sync.dma_start(
-                out=out[j // UNITS_PER_SERIES, :, first : first + PAIR, :].rearrange("s c k -> s (c k)"), in_=flat
+                out=out[series.start : series.stop, :, channel, :].rearrange("b s k -> s b k"), in_=result[:]
             )
 
-        for t in range(2 * SERIES):
-            start_trees(t)
-            finish_trees(t)
+        def quantise_steps(u):
+            grouped = n_grouped[u // 2][:, u % 2]
+            n_operand[u] = quantise(grouped.rearrange("p s w t -> p (s w t)"), P * len(series_of(u)), "n")
 
-        for i in range(-3, UNITS + 1):
-            if is_unit(i - 1):
-                sums1[i - 1] = multiply(nc, psum_acc, h_operand[i - 1], w1_codes, w1_planes, first_channel(i - 1), "acc1")
-            if is_unit(i):
-                add_first_bias(i)
-            if is_unit(i + 1):
-                n_operand[i + 1] = quantise(nc, work, n_grouped[i + 1], "n")
-            if is_unit(i - 1):
-                finish(i - 1)
-            if is_unit(i):
-                h_turned[i] = turn(nc, psum_tr, identity, h_rows[i])
-            if is_unit(i + 3):
-                subtract_and_turn(i + 3)
-            if is_unit(i + 1):
-                sums0[i + 1] = multiply(nc, psum_acc, n_operand[i + 1], w0_codes, w0_planes, first_channel(i + 1), "acc0")
-            if is_unit(i + 2):
-                n_grouped[i + 2] = gather_words(nc, ahead, n_turned[i + 2], ACT.Copy, "n")
-            if is_unit(i):
-                h_grouped[i] = gather_words(nc, work, h_turned[i], ACT.Relu, "h")
-            if is_unit(i):
-                h_operand[i] = quantise(nc, work, h_grouped[i], "h")
+        def quantise_filters(u):
+            h_operand[u] = quantise(h_grouped[u][:].rearrange("p n t -> p (n t)"), P * len(series_of(u)), "h")
+
+        def sums_on_vector(u):
+            return 2 if u >= UNITS - 2 else 0
+
+        def copies_on_scalar(u):
+            return 2 if u < 12 else 1
+
+        before = {
+            -1: ((turn_bias,),),
+            0: ((spread_midpoints, 1, 0,),),
+            3: ((spread_midpoints, 0, 1,),),
+            5: ((spread_midpoints, 1, 1,),),
+            7: ((spread_midpoints, 2, 0,),),
+            9: ((spread_midpoints, 3, 0,),),
+            11: ((spread_midpoints, 2, 1,),),
+            13: ((spread_midpoints, 3, 1,),),
+        }
+        behind = {
+            -2: ((start_trees, 1, 0,),),
+            -1: ((finish_trees, 1, 0,), (permute_first_weight, 2, 2,),),
+            1: ((start_trees, 0, 1,),),
+            2: ((finish_trees, 0, 1,),),
+            3: ((start_trees, 1, 1,),),
+            4: ((finish_trees, 1, 1,), (permute_first_weight, 4, 2,),),
+            5: ((permute_first_weight, 6, 2,), (start_trees, 2, 0,),),
+            6: ((finish_trees, 2, 0,),),
+            7: ((start_trees, 3, 0,),),
+            8: ((finish_trees, 3, 0,),),
+            9: ((start_trees, 2, 1,),),
+            10: ((finish_trees, 2, 1,),),
+            11: ((start_trees, 3, 1,),),
+            12: ((finish_trees, 3, 1,),),
+        }
+        stages = (
+            (turn_back, 1),
+            (turn_steps, -4),
+            (quantise_filters, 0),
+            (second_layer, 0),
+            (subtract, -3),
+            (interleave, -1),
+            (store, 1),
+            (finish_second, 0),
+            (quantise_steps, -2),
+            (first_layer, -2),
+            (finish_first, -2),
+        )
+        start_trees(0, 0)
+        finish_trees(0, 0)
+        spread_midpoints(0, 0)
+        permute_first_scales()
+        permute_first_weight(0, 2)
+        for i in range(-4, UNITS + 2):
+            for call in before.get(i, ()):
+                call[0](*call[1:])
+            for stage, lag in stages:
+                if 0 <= i - lag < UNITS:
+                    stage(i - lag)
+            for call in behind.get(i, ()):
+                call[0](*call[1:])

@@ -111,7 +111,7 @@ def tile_shapeletencoder_pa_e_kernel(tc, x, W0_words, W0_scales, b0, W1_words, W
         load_codes(nc, w1_codes, W1_words, HALF)
 
         tree_top = {}
-        neg_mid = {}
+        extremes = {}
         mid_rows = {}
         b1_columns = const.tile([P, CHANNELS, PACK], F32, name="b1_columns")
         xt = {}
@@ -156,24 +156,23 @@ def tile_shapeletencoder_pa_e_kernel(tc, x, W0_words, W0_scales, b0, W1_words, W
             nc.vector.tensor_reduce(
                 out=bottom[:], in_=low[:].rearrange("p (l c) -> p c l", c=HALF), axis=mybir.AxisListType.X, op=ALU.min
             )
-            total = small.tile([P, HALF], F32, name="total")
-            nc.vector.tensor_tensor(out=total[:], in0=top[:], in1=bottom[:], op=ALU.add)
-            neg_mid[s, half] = small.tile([P, HALF], F32, name="neg_mid")
-            nc.vector.tensor_scalar(out=neg_mid[s, half][:], in0=total[:], scalar1=-0.5, scalar2=None, op0=ALU.mult)
+            extremes[s, half] = small.tile([P, HALF], F32, name="extremes")
+            nc.vector.tensor_tensor(out=extremes[s, half][:], in0=top[:], in1=bottom[:], op=ALU.add)
 
         def spread_midpoints(s, half):
             spread = psum_xt.tile([P, HALF, P], F32, name="turned")
             for c in range(HALF):
-                nc.tensor.transpose(spread[:, c, :], neg_mid[s, half][:, c : c + 1].to_broadcast([P, P]), identity[:])
+                nc.tensor.transpose(spread[:, c, :], extremes[s, half][:, c : c + 1].to_broadcast([P, P]), identity[:])
             rows = small.tile([P, HALF, P], F32, name="mid_rows")
-            nc.scalar.copy(out=rows[:], in_=spread[:])
+            nc.scalar.activation(out=rows[:], in_=spread[:], func=ACT.Copy, scale=-0.5)
             mid_rows[s, half] = rows
 
         def permute_first_weight(first, count):
-            nc.vector.tensor_copy(
-                out=w0_codes[:, first : first + count, :].bitcast(I32).rearrange("p c (t m) -> p c t m", t=PACK),
-                in_=w0_raw[:, first : first + count, :].bitcast(I32).rearrange("p c (m t) -> p c t m", t=PACK),
-            )
+            for c in range(first, first + count):
+                nc.vector.tensor_copy(
+                    out=w0_codes[:, c, :].bitcast(I32).rearrange("p (t b i) -> p b t i", t=PACK, i=4),
+                    in_=w0_raw[:, c, :].bitcast(I32).rearrange("p (b i t) -> p b t i", t=PACK, i=4),
+                )
 
         def permute_first_scales():
             nc.vector.tensor_copy(
@@ -266,7 +265,10 @@ def tile_shapeletencoder_pa_e_kernel(tc, x, W0_words, W0_scales, b0, W1_words, W
 
         def interleave(u):
             h_grouped[u] = work.tile([P, P * len(series_of(u)), PACK], BF16, name="h_grouped", align_bytes=64)
-            nc.vector.tensor_copy(out=h_grouped[u][:], in_=h_rows[u][:].rearrange("p t n -> p n t"))
+            nc.vector.tensor_copy(
+                out=h_grouped[u][:].rearrange("p (b i) t -> p b t i", i=4),
+                in_=h_rows[u][:].rearrange("p t (b i) -> p b t i", i=4),
+            )
 
         def second_layer(u):
             channel = channel_of(u)

@@ -18,6 +18,7 @@ CHANNELS = 8
 K = 512
 PACK = 4
 HALF = 4
+PIECES = 2
 TREE_LEVELS = 4
 
 RUNS = ((0, 1, 0), (1, 1, 0), (0, 2, 1), (2, 2, 0), (2, 2, 1))
@@ -77,13 +78,16 @@ def tile_shapeletencoder_pa_e_kernel(tc, x, W0_words, W0_scales, b0, W1_words, W
 
         identity = const.tile([P, P], F32, name="identity")
         make_identity(nc, identity[:])
+        identity_bf16 = const.tile([P, P], BF16, name="identity_bf16")
+        make_identity(nc, identity_bf16[:])
 
         w0_raw = const.tile([P, CHANNELS, K], U32, name="w0_raw", align_bytes=64)
         w0_codes = const.tile([P, CHANNELS, K], U32, name="w0_codes", align_bytes=64)
         w1_codes = const.tile([P, CHANNELS, K], U32, name="w1_codes", align_bytes=64)
         w0_planes = const.tile([P, CHANNELS // HALF, K], U8, name="w0_planes", align_bytes=64)
-        b0_columns = const.tile([P, CHANNELS, PACK], BF16, name="b0_columns")
+        b0_rows = const.tile([P, K], BF16, name="b0_rows")
         b1_rows = const.tile([P, P], BF16, name="b1_rows")
+        nc.vector.memset(b0_rows[:], 0.0)
         nc.vector.memset(b1_rows[:], 0.0)
 
         x_tiles = []
@@ -97,12 +101,12 @@ def tile_shapeletencoder_pa_e_kernel(tc, x, W0_words, W0_scales, b0, W1_words, W
                 columns = slice(width * piece, width * (piece + 1))
                 nc.sync.dma_start(out=x_tiles[s][:, columns], in_=cells[:, columns])
 
-        load_series(0, 2)
+        load_series(0, PIECES)
         w0_raw_planes = load_planes(nc, const, W0_scales, "w0_raw")
+        nc.sync.dma_start(out=b0_rows[0:CHANNELS, :], in_=b0)
+        nc.sync.dma_start(out=b1_rows[0 : CHANNELS * PACK, :], in_=b1.rearrange("c (j p) -> (c j) p", p=P))
         load_codes(nc, w0_raw, W0_words, 0)
         load_series(1, 1)
-        nc.sync.dma_start(out=b0_columns[:], in_=b0.rearrange("c (p t) -> p c t", t=PACK))
-        nc.sync.dma_start(out=b1_rows[0 : CHANNELS * PACK, :], in_=b1.rearrange("c (j p) -> (c j) p", p=P))
         w1_planes = load_planes(nc, const, W1_scales, "w1")
         load_codes(nc, w1_codes, W1_words, 0)
         load_codes(nc, w0_raw, W0_words, HALF)
@@ -113,6 +117,7 @@ def tile_shapeletencoder_pa_e_kernel(tc, x, W0_words, W0_scales, b0, W1_words, W
         tree_top = {}
         extremes = {}
         mid_rows = {}
+        b0_columns = const.tile([P, CHANNELS, PACK], F32, name="b0_columns")
         b1_columns = const.tile([P, CHANNELS, PACK], F32, name="b1_columns")
         xt = {}
         n_grouped = {}
@@ -136,11 +141,12 @@ def tile_shapeletencoder_pa_e_kernel(tc, x, W0_words, W0_scales, b0, W1_words, W
                 tree.tile([P, HALF * K // 2], BF16, name="high0"),
                 tree.tile([P, HALF * K // 2], BF16, name="low0"),
             )
-            for part in range(2):
-                quarters = [mine[:, K // 4 * q : K // 4 * (q + 1), :] for q in (2 * part, 2 * part + 1)]
-                columns = slice(HALF * K // 4 * part, HALF * K // 4 * (part + 1))
+            steps_of_half = K // PIECES // 2
+            for part in range(PIECES):
+                ends = [mine[:, steps_of_half * q : steps_of_half * (q + 1), :] for q in (2 * part, 2 * part + 1)]
+                columns = slice(HALF * steps_of_half * part, HALF * steps_of_half * (part + 1))
                 for tops, op in zip(tree_top[s, half], (ALU.max, ALU.min)):
-                    nc.vector.tensor_tensor(out=by_step(tops[:, columns]), in0=quarters[0], in1=quarters[1], op=op)
+                    nc.vector.tensor_tensor(out=by_step(tops[:, columns]), in0=ends[0], in1=ends[1], op=op)
 
         def finish_trees(s, half):
             high, low = tree_top[s, half]
@@ -159,12 +165,15 @@ def tile_shapeletencoder_pa_e_kernel(tc, x, W0_words, W0_scales, b0, W1_words, W
             extremes[s, half] = small.tile([P, HALF], F32, name="extremes")
             nc.vector.tensor_tensor(out=extremes[s, half][:], in0=top[:], in1=bottom[:], op=ALU.add)
 
-        def spread_midpoints(s, half):
+        def spread_midpoints(s, half, at_once=HALF):
             spread = psum_xt.tile([P, HALF, P], F32, name="turned")
-            for c in range(HALF):
-                nc.tensor.transpose(spread[:, c, :], extremes[s, half][:, c : c + 1].to_broadcast([P, P]), identity[:])
             rows = small.tile([P, HALF, P], F32, name="mid_rows")
-            nc.scalar.activation(out=rows[:], in_=spread[:], func=ACT.Copy, scale=-0.5)
+            for first in range(0, HALF, at_once):
+                taken = slice(first, first + at_once)
+                for c in range(first, first + at_once):
+                    column = extremes[s, half][:, c : c + 1]
+                    nc.tensor.transpose(spread[:, c, :], column.to_broadcast([P, P]), identity[:])
+                nc.scalar.activation(out=rows[:, taken, :], in_=spread[:, taken, :], func=ACT.Copy, scale=-0.5)
             mid_rows[s, half] = rows
 
         def permute_first_weight(first, count):
@@ -174,18 +183,20 @@ def tile_shapeletencoder_pa_e_kernel(tc, x, W0_words, W0_scales, b0, W1_words, W
                     in_=w0_raw[:, c, :].bitcast(I32).rearrange("p (b i t) -> p b t i", t=PACK, i=4),
                 )
 
-        def permute_first_scales():
+        def permute_first_scales(h):
             nc.vector.tensor_copy(
-                out=w0_planes[:].rearrange("p h (t m) -> p h t m", t=PACK),
-                in_=w0_raw_planes[:].rearrange("p h (m t) -> p h t m", t=PACK),
+                out=w0_planes[:, h, :].rearrange("p (t m) -> p t m", t=PACK),
+                in_=w0_raw_planes[:, h, :].rearrange("p (m t) -> p t m", t=PACK),
             )
 
-        def turn_bias():
-            b1_wide = const.tile([P, P], F32, name="b1_wide")
-            nc.scalar.copy(out=b1_wide[:], in_=b1_rows[:])
-            b1_turned = psum_xt.tile([P, P], F32, name="turned")
-            nc.tensor.transpose(b1_turned[:], b1_wide[:], identity[:])
-            nc.scalar.copy(out=b1_columns[:].rearrange("p c j -> p (c j)"), in_=b1_turned[:, 0 : CHANNELS * PACK])
+        def turn_biases():
+            turned = psum_out.tile([P, PACK + 1, P], BF16, name="turned_out")
+            by_residue = b0_rows[:].rearrange("c (p t) -> c t p", t=PACK)
+            for t in range(PACK):
+                nc.tensor.transpose(turned[:, t, :], by_residue[:, t, :], identity_bf16[:])
+            nc.tensor.transpose(turned[:, PACK, :], b1_rows[:], identity_bf16[:])
+            nc.scalar.copy(out=b0_columns[:], in_=turned[:, 0:PACK, 0:CHANNELS].rearrange("p t c -> p c t"))
+            nc.scalar.copy(out=b1_columns[:].rearrange("p c j -> p (c j)"), in_=turned[:, PACK, 0 : CHANNELS * PACK])
 
         def is_unit(u):
             return 0 <= u < UNITS
@@ -300,9 +311,12 @@ def tile_shapeletencoder_pa_e_kernel(tc, x, W0_words, W0_scales, b0, W1_words, W
                     nc.vector.tensor_copy(out=result[:, member, :], in_=turned_out[u][member][:])
                 else:
                     nc.scalar.copy(out=result[:, member, :], in_=turned_out[u][member][:])
-            nc.sync.dma_start(
-                out=out[series.start : series.stop, :, channel, :].rearrange("b s k -> s b k"), in_=result[:]
-            )
+            at_once = 1 if u == UNITS - 1 else len(series)
+            for member in range(0, len(series), at_once):
+                rows = out[series.start + member : series.start + member + at_once, :, channel, :]
+                nc.sync.dma_start(
+                    out=rows.rearrange("b s k -> s b k"), in_=result[:, member : member + at_once, :]
+                )
 
         def quantise_steps(u):
             grouped = n_grouped[u // 2][:, u % 2]
@@ -318,8 +332,8 @@ def tile_shapeletencoder_pa_e_kernel(tc, x, W0_words, W0_scales, b0, W1_words, W
             return 2 if u < 12 else 1
 
         before = {
-            -1: ((turn_bias,),),
-            0: ((spread_midpoints, 1, 0,),),
+            -2: ((turn_biases,),),
+            1: ((spread_midpoints, 1, 0,),),
             3: ((spread_midpoints, 0, 1,),),
             5: ((spread_midpoints, 1, 1,),),
             7: ((spread_midpoints, 2, 0,),),
@@ -328,11 +342,11 @@ def tile_shapeletencoder_pa_e_kernel(tc, x, W0_words, W0_scales, b0, W1_words, W
             13: ((spread_midpoints, 3, 1,),),
         }
         behind = {
-            -2: ((start_trees, 1, 0,),),
-            -1: ((finish_trees, 1, 0,), (permute_first_weight, 2, 2,),),
+            -1: ((permute_first_weight, 2, 2,), (start_trees, 1, 0,),),
+            0: ((finish_trees, 1, 0,),),
             1: ((start_trees, 0, 1,),),
             2: ((finish_trees, 0, 1,),),
-            3: ((start_trees, 1, 1,),),
+            3: ((start_trees, 1, 1,), (permute_first_scales, 1,),),
             4: ((finish_trees, 1, 1,), (permute_first_weight, 4, 2,),),
             5: ((permute_first_weight, 6, 2,), (start_trees, 2, 0,),),
             6: ((finish_trees, 2, 0,),),
@@ -356,16 +370,17 @@ def tile_shapeletencoder_pa_e_kernel(tc, x, W0_words, W0_scales, b0, W1_words, W
             (first_layer, -2),
             (finish_first, -2),
         )
+        turn_steps(0)
         start_trees(0, 0)
         finish_trees(0, 0)
-        spread_midpoints(0, 0)
-        permute_first_scales()
+        spread_midpoints(0, 0, 2)
+        permute_first_scales(0)
         permute_first_weight(0, 2)
         for i in range(-4, UNITS + 2):
             for call in before.get(i, ()):
                 call[0](*call[1:])
             for stage, lag in stages:
-                if 0 <= i - lag < UNITS:
+                if 0 <= i - lag < UNITS and not (stage == turn_steps and i - lag == 0):
                     stage(i - lag)
             for call in behind.get(i, ()):
                 call[0](*call[1:])

@@ -307,10 +307,7 @@ def tile_shapeletencoder_pa_e_kernel(tc, x, W0_words, W0_scales, b0, W1_words, W
             series = series_of(u)
             result = results.tile([P, len(series), K], F32, name="result")
             for member in range(len(series)):
-                if member >= copies_on_scalar(u):
-                    nc.vector.tensor_copy(out=result[:, member, :], in_=turned_out[u][member][:])
-                else:
-                    nc.scalar.copy(out=result[:, member, :], in_=turned_out[u][member][:])
+                nc.any.tensor_copy(out=result[:, member, :], in_=turned_out[u][member][:])
             at_once = 1 if u == UNITS - 1 else len(series)
             for member in range(0, len(series), at_once):
                 rows = out[series.start + member : series.start + member + at_once, :, channel, :]
@@ -327,9 +324,6 @@ def tile_shapeletencoder_pa_e_kernel(tc, x, W0_words, W0_scales, b0, W1_words, W
 
         def sums_on_vector(u):
             return 2 if u >= UNITS - 2 else 0
-
-        def copies_on_scalar(u):
-            return 2 if u < 12 else 1
 
         before = {
             -2: ((turn_biases,),),

from contextlib import ExitStack

import concourse.mybir as mybir
from concourse.masks import make_identity

BF16 = mybir.dt.bfloat16
F32 = mybir.dt.float32
I32 = mybir.dt.int32
U32 = mybir.dt.uint32
U8 = mybir.dt.uint8
FP8X4 = mybir.dt.float8_e4m3fn_x4
ALU = mybir.AluOpType
ACT = mybir.ActivationFunctionType

P = 128
SERIES = 4
CHANNELS = 8
K = 512
PACK = 4
HALF = 4
PIECES = 2
TREE_LEVELS = 4

RUNS = ((0, 1, 0), (1, 1, 0), (0, 2, 1), (2, 2, 0), (2, 2, 1))
UNITS = HALF * len(RUNS)
BLOCKS = UNITS // 2

FLOPS = 2 * 2 * SERIES * P * CHANNELS * K * K


def load_planes(nc, pool, scales, label):
    planes = pool.tile([P, CHANNELS // HALF, K], U8, name=label + "_planes", align_bytes=64)
    nc.vector.memset(planes[:].bitcast(I32), 0)
    for h in range(CHANNELS // HALF):
        for quadrant in range(4):
            nc.sync.dma_start(
                out=planes[32 * quadrant : 32 * quadrant + 4 * HALF, h, :].bitcast(I32),
                in_=scales[HALF * h : HALF * h + HALF, 4 * quadrant : 4 * quadrant + 4, :].bitcast(I32),
            )
    return planes


def load_codes(nc, codes, words, first):
    nc.sync.dma_start(
        out=codes[:, first : first + HALF, :].bitcast(I32),
        in_=words[first : first + HALF].rearrange("g p n t -> p g (n t)").bitcast(I32),
    )


def halve(nc, tree, high, low, width, level):
    high_next = tree.tile([P, width], BF16, name="high%d" % level)
    low_next = tree.tile([P, width], BF16, name="low%d" % level)
    nc.vector.tensor_tensor(out=by_step(high_next[:]), in0=high[0], in1=high[1], op=ALU.max)
    nc.vector.tensor_tensor(out=by_step(low_next[:]), in0=low[0], in1=low[1], op=ALU.min)
    return high_next, low_next


def by_step(ap):
    return ap.rearrange("p (l c) -> p l c", c=HALF)


def halves(tile_ap, width):
    return by_step(tile_ap[:, 0:width]), by_step(tile_ap[:, width : 2 * width])


def tile_shapeletencoder_pa_e_kernel(tc, x, W0_words, W0_scales, b0, W1_words, W1_scales, b1, out):
    nc = tc.nc
    with ExitStack() as ctx:
        const = ctx.enter_context(tc.tile_pool(name="const", bufs=1))
        series_pool = ctx.enter_context(tc.tile_pool(name="series", bufs=SERIES))
        tree = ctx.enter_context(tc.tile_pool(name="tree", bufs=2))
        small = ctx.enter_context(tc.tile_pool(name="small", bufs=2 * SERIES))
        work = ctx.enter_context(tc.tile_pool(name="work", bufs=5))
        results = ctx.enter_context(tc.tile_pool(name="results", bufs=4))
        psum_xt = ctx.enter_context(tc.psum_pool(name="psum_xt", bufs=2))
        psum_acc = ctx.enter_context(tc.psum_pool(name="psum_acc", bufs=2))
        psum_out = ctx.enter_context(tc.psum_pool(name="psum_out", bufs=2))

        identity = const.tile([P, P], F32, name="identity")
        make_identity(nc, identity[:])
        identity_bf16 = const.tile([P, P], BF16, name="identity_bf16")
        make_identity(nc, identity_bf16[:])

        w0_raw = const.tile([P, CHANNELS, K], U32, name="w0_raw", align_bytes=64)
        w0_codes = const.tile([P, CHANNELS, K], U32, name="w0_codes", align_bytes=64)
        w1_codes = const.tile([P, CHANNELS, K], U32, name="w1_codes", align_bytes=64)
        w0_planes = const.tile([P, CHANNELS // HALF, K], U8, name="w0_planes", align_bytes=64)
        b0_rows = const.tile([P, K], BF16, name="b0_rows")
        b1_rows = const.tile([P, P], BF16, name="b1_rows")
        nc.vector.memset(b0_rows[:], 0.0)
        nc.vector.memset(b1_rows[:], 0.0)

        x_tiles = []
        for s in range(SERIES):
            x_tiles.append(series_pool.tile([P, K * CHANNELS], BF16, name="x_tile"))

        def load_series(s, pieces):
            width = K * CHANNELS // pieces
            cells = x[s].rearrange("(s l) c -> s (l c)", l=K)
            for piece in range(pieces):
                columns = slice(width * piece, width * (piece + 1))
                nc.sync.dma_start(out=x_tiles[s][:, columns], in_=cells[:, columns])

        load_series(0, PIECES)
        w0_raw_planes = load_planes(nc, const, W0_scales, "w0_raw")
        nc.sync.dma_start(out=b0_rows[0:CHANNELS, :], in_=b0)
        nc.sync.dma_start(out=b1_rows[0 : CHANNELS * PACK, :], in_=b1.rearrange("c (j p) -> (c j) p", p=P))
        load_codes(nc, w0_raw, W0_words, 0)
        load_series(1, 1)
        w1_planes = load_planes(nc, const, W1_scales, "w1")
        load_codes(nc, w1_codes, W1_words, 0)
        load_codes(nc, w0_raw, W0_words, HALF)
        load_series(2, 1)
        load_series(3, 1)
        load_codes(nc, w1_codes, W1_words, HALF)

        tree_top = {}
        extremes = {}
        mid_rows = {}
        b0_columns = const.tile([P, CHANNELS, PACK], F32, name="b0_columns")
        b1_columns = const.tile([P, CHANNELS, PACK], F32, name="b1_columns")
        xt = {}
        n_grouped = {}
        n_operand = {}
        sums0 = {}
        h_rows = {}
        h_grouped = {}
        h_operand = {}
        sums1 = {}
        features = {}
        turned_out = {}

        def start_trees(s, half):
            steps = x_tiles[s][:].rearrange("p (l c) -> p l c", c=CHANNELS)
            mine = steps[:, :, HALF * half : HALF * half + HALF]
            if s > 0:
                pair_of_halves = (mine[:, 0 : K // 2, :], mine[:, K // 2 : K, :])
                tree_top[s, half] = halve(nc, tree, pair_of_halves, pair_of_halves, HALF * K // 2, 0)
                return
            tree_top[s, half] = (
                tree.tile([P, HALF * K // 2], BF16, name="high0"),
                tree.tile([P, HALF * K // 2], BF16, name="low0"),
            )
            steps_of_half = K // PIECES // 2
            for part in range(PIECES):
                ends = [mine[:, steps_of_half * q : steps_of_half * (q + 1), :] for q in (2 * part, 2 * part + 1)]
                columns = slice(HALF * steps_of_half * part, HALF * steps_of_half * (part + 1))
                for tops, op in zip(tree_top[s, half], (ALU.max, ALU.min)):
                    nc.vector.tensor_tensor(out=by_step(tops[:, columns]), in0=ends[0], in1=ends[1], op=op)

        def finish_trees(s, half):
            high, low = tree_top[s, half]
            width = HALF * K // 2
            for level in range(1, TREE_LEVELS):
                width //= 2
                high, low = halve(nc, tree, halves(high, width), halves(low, width), width, level)
            top = small.tile([P, HALF], F32, name="top")
            bottom = small.tile([P, HALF], F32, name="bottom")
            nc.vector.tensor_reduce(
                out=top[:], in_=high[:].rearrange("p (l c) -> p c l", c=HALF), axis=mybir.AxisListType.X, op=ALU.max
            )
            nc.vector.tensor_reduce(
                out=bottom[:], in_=low[:].rearrange("p (l c) -> p c l", c=HALF), axis=mybir.AxisListType.X, op=ALU.min
            )
            extremes[s, half] = small.tile([P, HALF], F32, name="extremes")
            nc.vector.tensor_tensor(out=extremes[s, half][:], in0=top[:], in1=bottom[:], op=ALU.add)

        def spread_midpoints(s, half, at_once=HALF):
            spread = psum_xt.tile([P, HALF, P], F32, name="turned")
            rows = small.tile([P, HALF, P], F32, name="mid_rows")
            for first in range(0, HALF, at_once):
                taken = slice(first, first + at_once)
                for c in range(first, first + at_once):
                    column = extremes[s, half][:, c : c + 1]
                    nc.tensor.transpose(spread[:, c, :], column.to_broadcast([P, P]), identity[:])
                nc.scalar.activation(out=rows[:, taken, :], in_=spread[:, taken, :], func=ACT.Copy, scale=-0.5)
            mid_rows[s, half] = rows

        def permute_first_weight(first, count):
            for c in range(first, first + count):
                nc.vector.tensor_copy(
                    out=w0_codes[:, c, :].bitcast(I32).rearrange("p (t b i) -> p b t i", t=PACK, i=4),
                    in_=w0_raw[:, c, :].bitcast(I32).rearrange("p (b i t) -> p b t i", t=PACK, i=4),
                )

        def permute_first_scales(h):
            nc.vector.tensor_copy(
                out=w0_planes[:, h, :].rearrange("p (t m) -> p t m", t=PACK),
                in_=w0_raw_planes[:, h, :].rearrange("p (m t) -> p t m", t=PACK),
            )

        def turn_biases():
            turned = psum_out.tile([P, PACK + 1, P], BF16, name="turned_out")
            by_residue = b0_rows[:].rearrange("c (p t) -> c t p", t=PACK)
            for t in range(PACK):
                nc.tensor.transpose(turned[:, t, :], by_residue[:, t, :], identity_bf16[:])
            nc.tensor.transpose(turned[:, PACK, :], b1_rows[:], identity_bf16[:])
            nc.scalar.copy(out=b0_columns[:], in_=turned[:, 0:PACK, 0:CHANNELS].rearrange("p t c -> p c t"))
            nc.scalar.copy(out=b1_columns[:].rearrange("p c j -> p (c j)"), in_=turned[:, PACK, 0 : CHANNELS * PACK])

        def is_unit(u):
            return 0 <= u < UNITS

        def series_of(u):
            first, count, half = RUNS[u // HALF]
            return range(first, first + count)

        def channel_of(u):
            return HALF * RUNS[u // HALF][2] + u % HALF

        def series_of_turn(u):
            return series_of(u)[u % 2 : u % 2 + 1]

        def turn_steps(u):
            pair = channel_of(u) // 2
            for s in series_of_turn(u):
                words = x_tiles[s][:].bitcast(F32).rearrange("p (q t c) -> p t c q", t=PACK, c=CHANNELS // 2)
                xt[u] = psum_xt.tile([P, PACK, P], F32, name="turned")
                for t in range(PACK):
                    nc.tensor.transpose(xt[u][:, t, :], words[:, t, pair, :], identity[:])

        def subtract(u):
            half, first = divmod(channel_of(u - u % 2), HALF)
            if u % 2 == 0:
                n_grouped[u // 2] = work.tile([P, 2, len(series_of(u)), P, PACK], BF16, name="n_grouped", align_bytes=64)
            for s in series_of_turn(u):
                nc.vector.tensor_tensor(
                    out=n_grouped[u // 2][:, :, u % 2, :, :],
                    in0=xt[u][:].bitcast(BF16).rearrange("p t (w e) -> p e w t", e=2),
                    in1=mid_rows[s, half][:, first : first + 2, :].unsqueeze(3).to_broadcast([P, 2, P, PACK]),
                    op=ALU.add,
                )

        def quantise(grouped_flat, columns, label):
            codes = work.tile([P, columns], U32, name=label + "_codes", align_bytes=64)
            plane = work.tile([P, columns], U8, name=label + "_plane", align_bytes=64)
            nc.vector.quantize_mx(out=codes[:].bitcast(FP8X4), scales=plane[:], in_=grouped_flat)
            return codes, plane

        def multiply(weight_codes, weight_planes, channel, codes, plane, label):
            cells = codes.shape[1]
            fit = K // cells
            sums = []
            for first in range(0, PACK, fit):
                bank = psum_acc.tile([P, fit, cells], F32, name=label)
                for side in range(fit):
                    columns = slice(P * (first + side), P * (first + side + 1))
                    sums.append(bank[:, side, :])
                    nc.tensor.matmul_mx(
                        out=bank[:, side, :],
                        lhsT=weight_codes[:, channel, columns].bitcast(FP8X4),
                        lhsT_scale=weight_planes[4 * (channel % HALF) : P, channel // HALF, columns],
                        rhs=codes.bitcast(FP8X4),
                        rhs_scale=plane,
                        start=True,
                        stop=True,
                    )
            return sums

        def relu_with_bias(to, sums, column, on_vector):
            if on_vector:
                nc.vector.tensor_scalar(out=to, in0=sums, scalar1=column, scalar2=0.0, op0=ALU.add, op1=ALU.max)
            else:
                nc.scalar.activation(out=to, in_=sums, func=ACT.Relu, bias=column, scale=1.0)

        def first_layer(u):
            channel = channel_of(u)
            codes, plane = n_operand[u]
            sums0[u] = multiply(w0_codes, w0_planes, channel, codes[:], plane[:], "acc0")

        def finish_first(u):
            channel = channel_of(u)
            h_rows[u] = work.tile([P, PACK, P * len(series_of(u))], BF16, name="h_rows")
            for t in range(PACK):
                relu_with_bias(h_rows[u][:, t, :], sums0[u][t], b0_columns[:, channel, t : t + 1], t < sums_on_vector(u))

        def interleave(u):
            h_grouped[u] = work.tile([P, P * len(series_of(u)), PACK], BF16, name="h_grouped", align_bytes=64)
            nc.vector.tensor_copy(
                out=h_grouped[u][:].rearrange("p (b i) t -> p b t i", i=4),
                in_=h_rows[u][:].rearrange("p t (b i) -> p b t i", i=4),
            )

        def second_layer(u):
            channel = channel_of(u)
            codes, plane = h_operand[u]
            sums1[u] = multiply(w1_codes, w1_planes, channel, codes[:], plane[:], "acc1")

        def finish_second(u):
            channel = channel_of(u)
            features[u] = work.tile([P, PACK, P * len(series_of(u))], F32, name="features")
            for j in range(PACK):
                relu_with_bias(features[u][:, j, :], sums1[u][j], b1_columns[:, channel, j : j + 1], j < sums_on_vector(u))

        def turn_back(u):
            turned_out[u] = []
            for member in range(len(series_of(u))):
                bank = psum_out.tile([P, K], F32, name="turned_out")
                for j in range(PACK):
                    nc.tensor.transpose(
                        bank[:, P * j : P * (j + 1)], features[u][:, j, P * member : P * (member + 1)], identity[:]
                    )
                turned_out[u].append(bank)

        def store(u):
            channel = channel_of(u)
            series = series_of(u)
            result = results.tile([P, len(series), K], F32, name="result")
            for member in range(len(series)):
                nc.any.tensor_copy(out=result[:, member, :], in_=turned_out[u][member][:])
            at_once = 1 if u == UNITS - 1 else len(series)
            for member in range(0, len(series), at_once):
                rows = out[series.start + member : series.start + member + at_once, :, channel, :]
                nc.sync.dma_start(
                    out=rows.rearrange("b s k -> s b k"), in_=result[:, member : member + at_once, :]
                )

        def quantise_steps(u):
            grouped = n_grouped[u // 2][:, u % 2]
            n_operand[u] = quantise(grouped.rearrange("p s w t -> p (s w t)"), P * len(series_of(u)), "n")

        def quantise_filters(u):
            h_operand[u] = quantise(h_grouped[u][:].rearrange("p n t -> p (n t)"), P * len(series_of(u)), "h")

        def sums_on_vector(u):
            return 2 if u >= UNITS - 2 else 0

        before = {
            -2: ((turn_biases,),),
            1: ((spread_midpoints, 1, 0,),),
            3: ((spread_midpoints, 0, 1,),),
            5: ((spread_midpoints, 1, 1,),),
            7: ((spread_midpoints, 2, 0,),),
            9: ((spread_midpoints, 3, 0,),),
            11: ((spread_midpoints, 2, 1,),),
            13: ((spread_midpoints, 3, 1,),),
        }
        behind = {
            -1: ((permute_first_weight, 2, 2,), (start_trees, 1, 0,),),
            0: ((finish_trees, 1, 0,),),
            1: ((start_trees, 0, 1,),),
            2: ((finish_trees, 0, 1,),),
            3: ((start_trees, 1, 1,), (permute_first_scales, 1,),),
            4: ((finish_trees, 1, 1,), (permute_first_weight, 4, 2,),),
            5: ((permute_first_weight, 6, 2,), (start_trees, 2, 0,),),
            6: ((finish_trees, 2, 0,),),
            7: ((start_trees, 3, 0,),),
            8: ((finish_trees, 3, 0,),),
            9: ((start_trees, 2, 1,),),
            10: ((finish_trees, 2, 1,),),
            11: ((start_trees, 3, 1,),),
            12: ((finish_trees, 3, 1,),),
        }
        stages = (
            (turn_back, 1),
            (turn_steps, -4),
            (quantise_filters, 0),
            (second_layer, 0),
            (subtract, -3),
            (interleave, -1),
            (store, 1),
            (finish_second, 0),
            (quantise_steps, -2),
            (first_layer, -2),
            (finish_first, -2),
        )
        turn_steps(0)
        start_trees(0, 0)
        finish_trees(0, 0)
        spread_midpoints(0, 0, 2)
        permute_first_scales(0)
        permute_first_weight(0, 2)
        for i in range(-4, UNITS + 2):
            for call in before.get(i, ()):
                call[0](*call[1:])
            for stage, lag in stages:
                if 0 <= i - lag < UNITS and not (stage == turn_steps and i - lag == 0):
                    stage(i - lag)
            for call in behind.get(i, ()):
                call[0](*call[1:])
